import numpy as np
import ml_dtypes


def mxq(x, axis, fmt="e4m3"):
    dtype, down = {"e4m3": (ml_dtypes.float8_e4m3fn, 7), "e5m2": (ml_dtypes.float8_e5m2, 14)}[fmt]
    v = np.moveaxis(np.asarray(x, np.float32).astype(ml_dtypes.bfloat16).astype(np.float64), axis, -1)
    blocks = v.reshape(v.shape[:-1] + (-1, 32))
    amax = np.abs(blocks).max(-1, keepdims=True)
    byte = np.maximum(np.where(amax > 0, np.frexp(amax)[1] - 1 + 127, 0) - down, 1)
    scale = np.exp2(byte - 127.0)
    codes = (blocks / scale).astype(np.float32).astype(dtype).astype(np.float64)
    return np.moveaxis((codes * scale).reshape(v.shape), -1, axis)


WIDE = False


def mx_kscale(k):
    if not WIDE:
        return np.ones(k)
    levels = np.array([10, -10, 5, -5, 0])
    if k % 512:
        return np.exp2(np.random.permutation(np.resize(levels, k // 32))).repeat(32)
    a = np.empty((k // 512, 16))
    for p in range(k // 512):
        a[p, :8] = np.random.permutation(np.resize(levels, 8))
        for g in range(8):
            far = levels[np.abs(levels - a[p, g]) >= 10]
            a[p, g + 8] = far[np.random.randint(len(far))]
    return np.exp2(a.ravel()).repeat(32)


BF16 = ml_dtypes.bfloat16


def bf(x):
    return np.asarray(x, np.float32).astype(BF16)


def f64(x):
    return np.asarray(x).astype(np.float64)


E2M1 = np.array([0.0, 0.5, 1.0, 1.5, 2.0, 3.0, 4.0, 6.0, -0.0, -0.5, -1.0, -1.5, -2.0, -3.0, -4.0, -6.0])


def pack_weight(w, fmt):
    k, n = w.shape
    w = f64(bf(w)).reshape(k // 32, 32, n)
    amax = np.abs(w).max(1)
    if fmt == "e4m3":
        byte = np.frexp(amax)[1] - 1 + 127 - 7
    else:
        mant, ex = np.frexp(amax / 6.0)
        byte = np.where(mant > 0.5, ex, ex - 1) + 127
    byte = np.clip(np.where(amax > 0, byte, 1), 1, 254)
    scaled = (w * np.exp2(127.0 - byte)[:, None, :]).reshape(k, n).astype(np.float32)
    by_word = np.ascontiguousarray(scaled.reshape(k // 512, 128, 4, n).transpose(0, 1, 3, 2))
    if fmt == "e4m3":
        words = by_word.astype(ml_dtypes.float8_e4m3fn).view(np.uint8)
    else:
        c = by_word.astype(ml_dtypes.float4_e2m1fn).view(np.uint8) & 0xF
        words = c[..., 0::2] | (c[..., 1::2] << 4)
    return np.ascontiguousarray(words), np.ascontiguousarray(byte.astype(np.uint8).reshape(k // 512, 16, n))


def unpack_weight(words, scales, fmt):
    g, p, n, _ = words.shape
    if fmt == "e4m3":
        vals = np.ascontiguousarray(words).view(ml_dtypes.float8_e4m3fn).astype(np.float64)
    else:
        nib = np.empty((g, p, n, 4), np.uint8)
        nib[..., 0::2] = words & 0xF
        nib[..., 1::2] = words >> 4
        vals = E2M1[nib]
    vals = vals * np.repeat(np.exp2(scales.astype(np.float64) - 127.0), 8, axis=1)[..., None]
    return vals.transpose(0, 1, 3, 2).reshape(g * 512, n)


E, F, H, MID, OUT = 128, 2048, 6144, 512, 2048
D = 2 * (F + H)
IN = D + 1
FMT = "e4m3"


def setup_inputs():
    s = mx_kscale(D)
    t = mx_kscale(MID)
    w1 = np.concatenate([np.random.standard_normal((MID, D)) / np.sqrt(D) / s[None, :],
                         np.random.standard_normal((MID, 1)) * 0.5], axis=1) * t[:, None]
    dst_node_feat = bf(np.random.standard_normal((E, F)) * s[:F])
    dst_node_hidden = bf(np.random.standard_normal((E, H)) * s[F:F + H])
    src_node_feat = bf(np.random.standard_normal((E, F)) * s[F + H:2 * F + H])
    src_node_hidden = bf(np.random.standard_normal((E, H)) * s[2 * F + H:])
    edge_feat = bf(np.random.standard_normal(E))
    b1 = bf(np.random.standard_normal(MID) * 0.3 * t)
    w2 = np.random.standard_normal((OUT, MID)) / np.sqrt(MID) / t[None, :]
    w2_words, w2_scales = pack_weight(np.ascontiguousarray(w2.T), FMT)
    b2 = bf(np.random.standard_normal(OUT) * 0.3)
    return {"dst_node_feat": dst_node_feat,
            "dst_node_hidden": dst_node_hidden,
            "src_node_feat": src_node_feat,
            "src_node_hidden": src_node_hidden,
            "edge_feat": edge_feat,
            "W1": bf(w1),
            "b1": b1,
            "W2_words": w2_words,
            "W2_scales": w2_scales,
            "b2": b2}


def reference(dst_node_feat, dst_node_hidden, src_node_feat, src_node_hidden, edge_feat, W1, b1, W2_words, W2_scales, b2):
    x = np.concatenate([f64(dst_node_feat), f64(dst_node_hidden), f64(src_node_feat), f64(src_node_hidden),
                        f64(edge_feat)[:, None]], axis=1)
    w1 = f64(W1)
    pre = (mxq(x[:, :D], 1, "e4m3") @ mxq(w1[:, :D], 1, "e4m3").T) + x[:, D:] * w1[:, D] + f64(b1)
    h = np.maximum(pre, 0.0)
    return np.tanh((mxq(h, 1, "e4m3") @ unpack_weight(W2_words, W2_scales, FMT)) + f64(b2))

@@ -1,0 +1,232 @@
+from contextlib import ExitStack
+
+import concourse.mybir as mybir
+from concourse.masks import make_identity
+
+F32 = mybir.dt.float32
+BF16 = mybir.dt.bfloat16
+I32 = mybir.dt.int32
+U32 = mybir.dt.uint32
+U8 = mybir.dt.uint8
+FP8X4 = mybir.dt.float8_e4m3fn_x4
+ADD = mybir.AluOpType.add
+MULT = mybir.AluOpType.mult
+RELU = mybir.ActivationFunctionType.Relu
+TANH = mybir.ActivationFunctionType.Tanh
+
+P = 128
+PACK = 4
+K_PASS = P * PACK
+EDGES = 128
+NODE_K = 16384
+MID = 512
+OUT = 2048
+ROW_SETS = MID // P
+BANK = 512
+PSUM_BANKS = 8
+
+K_BANK = 2 * BANK
+BANK_PASSES = K_BANK // K_PASS
+UNIT_BANKS = 4
+K_UNIT = UNIT_BANKS * K_BANK
+UNIT_PASSES = K_UNIT // K_PASS
+ROW_UNITS = NODE_K // K_UNIT
+W_UNITS = ROW_SETS * ROW_UNITS
+W_BUFS = 8
+MX_LAG = 2
+
+FLOPS = 2 * EDGES * (NODE_K + 1) * MID + 2 * EDGES * MID * OUT
+
+
+def tile_edgenetwork_k_kernel(
+    tc,
+    dst_node_feat,
+    dst_node_hidden,
+    src_node_feat,
+    src_node_hidden,
+    edge_feat,
+    W1,
+    b1,
+    W2_words,
+    W2_scales,
+    b2,
+    out,
+):
+    nc = tc.nc
+    node_inputs = (dst_node_feat, dst_node_hidden, src_node_feat, src_node_hidden)
+    w1_sets = W1.rearrange("(p t) k -> t p k", t=ROW_SETS)
+
+    with ExitStack() as stack:
+        const = stack.enter_context(tc.tile_pool(name="const", bufs=1))
+        raw = stack.enter_context(tc.tile_pool(name="raw", bufs=W_BUFS))
+        grouped_pool = stack.enter_context(tc.tile_pool(name="grouped", bufs=3))
+        codes = stack.enter_context(tc.tile_pool(name="codes", bufs=MX_LAG + 2))
+        results = stack.enter_context(tc.tile_pool(name="results", bufs=OUT // BANK))
+        sums = stack.enter_context(tc.psum_pool(name="sums", bufs=1))
+        banks = stack.enter_context(tc.psum_pool(name="banks", bufs=PSUM_BANKS - 1))
+        stack.enter_context(tc.manual_schedule())
+
+        b1_bf = const.tile([P, ROW_SETS], BF16)
+        nc.scalar.dma_start(out=b1_bf[:], in_=b1.rearrange("(p t) -> p t", t=ROW_SETS))
+        w1_edge_bf = const.tile([P, ROW_SETS, 1], BF16)
+        with nc.allow_non_contiguous_dma(reason="one column of W1: 512 single elements"):
+            nc.scalar.dma_start(
+                out=w1_edge_bf[:], in_=W1.rearrange("(p t) k -> p t k", t=ROW_SETS)[:, :, NODE_K : NODE_K + 1]
+            )
+
+        one_row = const.tile([P, OUT + BANK], BF16)
+        nc.vector.memset(one_row[:].bitcast(I32), 0)
+        ones = const.tile([P, P], BF16)
+        nc.vector.memset(ones[:], 1.0)
+        w2_scales = const.tile([P, OUT], U8, align_bytes=64)
+        nc.vector.memset(w2_scales[:].bitcast(I32), 0)
+        warm = const.tile([P, 1], F32)
+        nc.vector.memset(warm[:], 0.0)
+        nc.scalar.activation(out=warm[:], in_=warm[:], func=TANH)
+        ident = const.tile([P, P], F32)
+        make_identity(nc, ident[:])
+
+        x_banks = []
+        for i, part in enumerate(node_inputs):
+            x_tile = const.tile([P, part.shape[1]], BF16, name="x_raw%d" % i)
+            nc.sync.dma_start(out=x_tile[:], in_=part)
+            x_banks.extend([x_tile[:].bitcast(F32)[:, j * BANK : (j + 1) * BANK] for j in range(part.shape[1] // K_BANK)])
+            if i == 0:
+                nc.sync.dma_start(out=one_row[0:1, 0:OUT], in_=b2.unsqueeze(0))
+                nc.sync.dma_start(out=one_row[0:1, OUT : OUT + EDGES], in_=edge_feat.unsqueeze(0))
+
+        w_raw = []
+
+        def load_w_unit(u):
+            t, kq = divmod(u, ROW_UNITS)
+            w_tile = raw.tile([P, K_UNIT], BF16)
+            nc.sync.dma_start(out=w_tile[:], in_=w1_sets[t][:, kq * K_UNIT : (kq + 1) * K_UNIT])
+            w_raw.append(w_tile)
+
+        for u in range(W_BUFS):
+            load_w_unit(u)
+
+        def quantise_unit(bank_pairs, unit_codes, unit_scales):
+            grouped = grouped_pool.tile([P, K_UNIT], BF16, align_bytes=64)
+            for j, pairs in enumerate(bank_pairs):
+                bank = banks.tile([P, 2 * BANK_PASSES, P], F32, tag="bank")
+                for b in range(2 * BANK_PASSES):
+                    g, u = divmod(b, 2)
+                    nc.tensor.transpose(bank[:, b, :], pairs[:, 2 * P * g + u : 2 * P * (g + 1) : 2], ident[:])
+                copy = nc.vector.tensor_copy if j == UNIT_BANKS - 1 else nc.scalar.copy
+                copy(
+                    out=grouped[:].bitcast(F32)[:, j * BANK : (j + 1) * BANK].rearrange(
+                        "p (g r u) -> p g r u", g=BANK_PASSES, u=2
+                    ),
+                    in_=bank[:].rearrange("p (g u) r -> p g r u", u=2),
+                )
+            for half in range(2):
+                words = slice(half * K_UNIT // PACK // 2, (half + 1) * K_UNIT // PACK // 2)
+                nc.vector.quantize_mx(
+                    out=unit_codes[:, words].bitcast(FP8X4),
+                    scales=unit_scales[:, words],
+                    in_=grouped[:, half * K_UNIT // 2 : (half + 1) * K_UNIT // 2],
+                )
+
+        every_row = const.tile([P, OUT + BANK], BF16)
+        b2_all = every_row[:, 0:OUT]
+        edge_all = every_row[:, OUT : OUT + EDGES]
+        added = const.tile([P, ROW_SETS, EDGES], F32)
+
+        def prepare_biases():
+            for n in range(OUT // BANK + 1):
+                cols = slice(n * BANK, (n + 1) * BANK)
+                spread = banks.tile([P, BANK], F32, tag="bank")
+                nc.tensor.matmul(out=spread[:], lhsT=ones[:], rhs=one_row[:, cols], start=True, stop=True)
+                nc.scalar.copy(out=every_row[:, cols], in_=spread[:])
+            b1_f32 = const.tile([P, ROW_SETS], F32)
+            nc.vector.tensor_copy(out=b1_f32[:], in_=b1_bf[:])
+            w1_edge = const.tile([P, ROW_SETS], F32)
+            nc.vector.tensor_copy(out=w1_edge[:], in_=w1_edge_bf[:, :, 0])
+            for t in range(ROW_SETS):
+                nc.vector.tensor_scalar(
+                    out=added[:, t, :],
+                    in0=edge_all,
+                    scalar1=w1_edge[:, t : t + 1],
+                    scalar2=b1_f32[:, t : t + 1],
+                    op0=MULT,
+                    op1=ADD,
+                )
+
+        x_codes = []
+        x_scales = []
+        for kq in range(ROW_UNITS):
+            x_unit_codes = const.tile([P, K_UNIT // PACK], U32, name="x_codes%d" % kq, align_bytes=64)
+            x_unit_scales = const.tile([P, K_UNIT // PACK], U8, name="x_scales%d" % kq, align_bytes=64)
+            quantise_unit(x_banks[kq * UNIT_BANKS : (kq + 1) * UNIT_BANKS], x_unit_codes, x_unit_scales)
+            x_codes.append(x_unit_codes)
+            x_scales.append(x_unit_scales)
+            if kq == 0:
+                prepare_biases()
+
+        pre = sums.tile([P, ROW_SETS, EDGES], F32)
+        h_grouped = const.tile([P, EDGES, PACK], BF16, align_bytes=64)
+
+        def multiply_unit(u, w_codes, w_scales):
+            t, kq = divmod(u, ROW_UNITS)
+            for i in range(UNIT_PASSES):
+                cols = slice(i * P, (i + 1) * P)
+                nc.tensor.matmul_mx(
+                    out=pre[:, t, :],
+                    lhsT=w_codes[:, cols].bitcast(FP8X4),
+                    lhsT_scale=w_scales[:, cols],
+                    rhs=x_codes[kq][:, cols].bitcast(FP8X4),
+                    rhs_scale=x_scales[kq][:, cols],
+                    start=(kq == 0 and i == 0),
+                    stop=(kq == ROW_UNITS - 1 and i == UNIT_PASSES - 1),
+                )
+            if kq == ROW_UNITS - 1:
+                h_f32 = results.tile([P, EDGES], F32)
+                nc.vector.tensor_tensor(out=h_f32[:], in0=pre[:, t, :], in1=added[:, t, :], op=ADD)
+                nc.scalar.activation(out=h_grouped[:, :, t], in_=h_f32[:], func=RELU)
+
+        quantised = []
+        for u in range(W_UNITS + MX_LAG):
+            if u < W_UNITS:
+                w_codes = codes.tile([P, K_UNIT // PACK], U32, align_bytes=64)
+                w_scales = codes.tile([P, K_UNIT // PACK], U8, align_bytes=64)
+                w_pairs = w_raw[u][:].bitcast(F32)
+                quantise_unit([w_pairs[:, j * BANK : (j + 1) * BANK] for j in range(UNIT_BANKS)], w_codes, w_scales)
+                quantised.append((w_codes, w_scales))
+            if u + W_BUFS < W_UNITS:
+                load_w_unit(u + W_BUFS)
+            if u >= MX_LAG:
+                multiply_unit(u - MX_LAG, *quantised[u - MX_LAG])
+
+        scale_rows = W2_scales[0].rearrange("(q r) n -> r q n", r=4)
+        for r in range(4):
+            nc.sync.dma_start(out=w2_scales[r:P:32, :].bitcast(I32), in_=scale_rows[r].bitcast(I32))
+        w2_codes = const.tile([P, OUT], U32, align_bytes=64)
+        w2_words = W2_words[0].rearrange("p n t -> p (n t)").bitcast(I32)
+        for n in range(OUT // BANK):
+            cols = slice(n * BANK, (n + 1) * BANK)
+            nc.sync.dma_start(out=w2_codes[:, cols].bitcast(I32), in_=w2_words[:, cols])
+
+        h_codes = const.tile([P, EDGES], U32, align_bytes=64)
+        h_scales = const.tile([P, EDGES], U8, align_bytes=64)
+        nc.vector.quantize_mx(
+            out=h_codes[:].bitcast(FP8X4), scales=h_scales[:], in_=h_grouped[:].rearrange("p e t -> p (e t)")
+        )
+
+        for n in range(OUT // BANK):
+            cols = slice(n * BANK, (n + 1) * BANK)
+            product = banks.tile([P, BANK], F32, tag="bank")
+            nc.tensor.matmul_mx(
+                out=product[:],
+                lhsT=h_codes[:].bitcast(FP8X4),
+                lhsT_scale=h_scales[:],
+                rhs=w2_codes[:, cols].bitcast(FP8X4),
+                rhs_scale=w2_scales[:, cols],
+                start=True,
+                stop=True,
+            )
+            biased = results.tile([P, BANK], F32)
+            nc.vector.tensor_tensor(out=biased[:], in0=product[:], in1=b2_all[:, cols], op=ADD)
+            y = results.tile([P, BANK], F32)
+            nc.scalar.activation(out=y[:], in_=biased[:], func=TANH)
+            nc.sync.dma_start(out=out[:, cols], in_=y[:])

@@ -22,20 +22,39 @@ NODE_K = 16384
 MID = 512
 OUT = 2048
 ROW_SETS = MID // P
+LAST = ROW_SETS - 1
 BANK = 512
 PSUM_BANKS = 8
+SUM_BANKS = 2
 
 K_BANK = 2 * BANK
 BANK_PASSES = K_BANK // K_PASS
+READS = 2 * BANK_PASSES
+QUANT_BANKS = 2
 UNIT_BANKS = 4
-K_UNIT = UNIT_BANKS * K_BANK
-UNIT_PASSES = K_UNIT // K_PASS
-ROW_UNITS = NODE_K // K_UNIT
-W_UNITS = ROW_SETS * ROW_UNITS
+X_BANKS = 2
+X_PIECES = NODE_K // K_BANK // X_BANKS
+X_PIECE_PASSES = X_BANKS * BANK_PASSES
+BIAS_PIECE = 1
+W_STRIDED = 1
 W_BUFS = 8
+ORDER_LEAD = 2
 MX_LAG = 2
 
 FLOPS = 2 * EDGES * (NODE_K + 1) * MID + 2 * EDGES * MID * OUT
+
+
+def w1_units():
+    units = []
+    for t in range(ROW_SETS):
+        sizes = [UNIT_BANKS] * (NODE_K // K_BANK // UNIT_BANKS)
+        if t == LAST:
+            sizes[-1:] = [UNIT_BANKS // 2] * 2
+        first = 0
+        for size in sizes:
+            units.append((t, first, size))
+            first += size
+    return units
 
 
 def tile_edgenetwork_k_kernel(
@@ -55,16 +74,29 @@ def tile_edgenetwork_k_kernel(
     nc = tc.nc
     node_inputs = (dst_node_feat, dst_node_hidden, src_node_feat, src_node_hidden)
     w1_sets = W1.rearrange("(p t) k -> t p k", t=ROW_SETS)
+    units = w1_units()
 
     with ExitStack() as stack:
         const = stack.enter_context(tc.tile_pool(name="const", bufs=1))
         raw = stack.enter_context(tc.tile_pool(name="raw", bufs=W_BUFS))
+        ordered_pool = stack.enter_context(tc.tile_pool(name="ordered", bufs=ORDER_LEAD + 2))
         grouped_pool = stack.enter_context(tc.tile_pool(name="grouped", bufs=3))
         codes = stack.enter_context(tc.tile_pool(name="codes", bufs=MX_LAG + 2))
-        results = stack.enter_context(tc.tile_pool(name="results", bufs=OUT // BANK))
+        results = stack.enter_context(tc.tile_pool(name="results", bufs=4))
         sums = stack.enter_context(tc.psum_pool(name="sums", bufs=1))
-        banks = stack.enter_context(tc.psum_pool(name="banks", bufs=PSUM_BANKS - 1))
+        banks = stack.enter_context(tc.psum_pool(name="banks", bufs=PSUM_BANKS - SUM_BANKS))
         stack.enter_context(tc.manual_schedule())
+
+        one_row = const.tile([P, OUT + EDGES], BF16)
+        nc.vector.memset(one_row[:].bitcast(I32), 0)
+        ones = const.tile([P, P], BF16)
+        nc.vector.memset(ones[:], 1.0)
+        warm = const.tile([P, 1], F32)
+        nc.vector.memset(warm[:], 0.0)
+        w2_scales = const.tile([P, OUT], U8, align_bytes=64)
+        nc.vector.memset(w2_scales[:].bitcast(I32), 0)
+        ident = const.tile([P, P], F32)
+        make_identity(nc, ident[:])
 
         b1_bf = const.tile([P, ROW_SETS], BF16)
         nc.scalar.dma_start(out=b1_bf[:], in_=b1.rearrange("(p t) -> p t", t=ROW_SETS))
@@ -73,72 +105,95 @@ def tile_edgenetwork_k_kernel(
             nc.scalar.dma_start(
                 out=w1_edge_bf[:], in_=W1.rearrange("(p t) k -> p t k", t=ROW_SETS)[:, :, NODE_K : NODE_K + 1]
             )
-
-        one_row = const.tile([P, OUT + BANK], BF16)
-        nc.vector.memset(one_row[:].bitcast(I32), 0)
-        ones = const.tile([P, P], BF16)
-        nc.vector.memset(ones[:], 1.0)
-        w2_scales = const.tile([P, OUT], U8, align_bytes=64)
-        nc.vector.memset(w2_scales[:].bitcast(I32), 0)
-        warm = const.tile([P, 1], F32)
-        nc.vector.memset(warm[:], 0.0)
         nc.scalar.activation(out=warm[:], in_=warm[:], func=TANH)
-        ident = const.tile([P, P], F32)
-        make_identity(nc, ident[:])
 
-        x_banks = []
+        def strided_reads(pairs):
+            return [pairs[:, 2 * P * g + u : 2 * P * (g + 1) : 2] for g in range(BANK_PASSES) for u in range(2)]
+
+        x_reads = []
         for i, part in enumerate(node_inputs):
             x_tile = const.tile([P, part.shape[1]], BF16, name="x_raw%d" % i)
-            nc.sync.dma_start(out=x_tile[:], in_=part)
-            x_banks.extend([x_tile[:].bitcast(F32)[:, j * BANK : (j + 1) * BANK] for j in range(part.shape[1] // K_BANK)])
+            first = 0
+            for width in (2 * K_BANK, part.shape[1] - 2 * K_BANK):
+                if width:
+                    nc.sync.dma_start(out=x_tile[:, first : first + width], in_=part[:, first : first + width])
+                    first += width
             if i == 0:
                 nc.sync.dma_start(out=one_row[0:1, 0:OUT], in_=b2.unsqueeze(0))
                 nc.sync.dma_start(out=one_row[0:1, OUT : OUT + EDGES], in_=edge_feat.unsqueeze(0))
+            for j in range(part.shape[1] // K_BANK):
+                x_reads.append(strided_reads(x_tile[:].bitcast(F32)[:, j * BANK : (j + 1) * BANK]))
 
         w_raw = []
 
-        def load_w_unit(u):
-            t, kq = divmod(u, ROW_UNITS)
-            w_tile = raw.tile([P, K_UNIT], BF16)
-            nc.sync.dma_start(out=w_tile[:], in_=w1_sets[t][:, kq * K_UNIT : (kq + 1) * K_UNIT])
-            w_raw.append(w_tile)
+        def load_next_unit():
+            if len(w_raw) < len(units):
+                t, first, size = units[len(w_raw)]
+                w_tile = raw.tile([P, UNIT_BANKS * K_BANK], BF16)
+                nc.sync.dma_start(
+                    out=w_tile[:, 0 : size * K_BANK], in_=w1_sets[t][:, first * K_BANK : (first + size) * K_BANK]
+                )
+                w_raw.append(w_tile[:].bitcast(F32))
 
         for u in range(W_BUFS):
-            load_w_unit(u)
+            load_next_unit()
 
-        def quantise_unit(bank_pairs, unit_codes, unit_scales):
-            grouped = grouped_pool.tile([P, K_UNIT], BF16, align_bytes=64)
-            for j, pairs in enumerate(bank_pairs):
-                bank = banks.tile([P, 2 * BANK_PASSES, P], F32, tag="bank")
-                for b in range(2 * BANK_PASSES):
-                    g, u = divmod(b, 2)
-                    nc.tensor.transpose(bank[:, b, :], pairs[:, 2 * P * g + u : 2 * P * (g + 1) : 2], ident[:])
-                copy = nc.vector.tensor_copy if j == UNIT_BANKS - 1 else nc.scalar.copy
+        w_reads = []
+
+        def order_next_unit():
+            if len(w_reads) < len(units):
+                size = units[len(w_reads)][2]
+                pairs = w_raw[len(w_reads)]
+                strided = W_STRIDED if size == UNIT_BANKS else size
+                reads = [strided_reads(pairs[:, j * BANK : (j + 1) * BANK]) for j in range(strided)]
+                if strided < size:
+                    ordered = ordered_pool.tile([P, (UNIT_BANKS - W_STRIDED) * BANK], F32)
+                    nc.vector.tensor_copy(
+                        out=ordered[:].rearrange("p (g u w) -> p g u w", u=2, w=P),
+                        in_=pairs[:, strided * BANK :].rearrange("p (g w u) -> p g u w", u=2, w=P),
+                    )
+                    for j in range(size - strided):
+                        reads.append([ordered[:, (j * READS + b) * P : (j * READS + b + 1) * P] for b in range(READS)])
+                w_reads.append(reads)
+
+        def quantise_banks(bank_reads, vector_banks, to_codes, to_scales):
+            size = len(bank_reads)
+            grouped = grouped_pool.tile([P, UNIT_BANKS * K_BANK], BF16, align_bytes=64)
+            for j, reads in enumerate(bank_reads):
+                bank = banks.tile([P, READS, P], F32, tag="bank")
+                for b, read in enumerate(reads):
+                    nc.tensor.transpose(bank[:, b, :], read, ident[:])
+                copy = nc.vector.tensor_copy if j in vector_banks else nc.scalar.copy
                 copy(
                     out=grouped[:].bitcast(F32)[:, j * BANK : (j + 1) * BANK].rearrange(
                         "p (g r u) -> p g r u", g=BANK_PASSES, u=2
                     ),
                     in_=bank[:].rearrange("p (g u) r -> p g r u", u=2),
                 )
-            for half in range(2):
-                words = slice(half * K_UNIT // PACK // 2, (half + 1) * K_UNIT // PACK // 2)
+            for j in range(0, size, QUANT_BANKS):
+                end = min(j + QUANT_BANKS, size)
+                words = slice(j * BANK_PASSES * P, end * BANK_PASSES * P)
                 nc.vector.quantize_mx(
-                    out=unit_codes[:, words].bitcast(FP8X4),
-                    scales=unit_scales[:, words],
-                    in_=grouped[:, half * K_UNIT // 2 : (half + 1) * K_UNIT // 2],
+                    out=to_codes[:, words].bitcast(FP8X4),
+                    scales=to_scales[:, words],
+                    in_=grouped[:, j * K_BANK : end * K_BANK],
                 )
 
-        every_row = const.tile([P, OUT + BANK], BF16)
+        every_row = const.tile([P, OUT + EDGES], BF16)
         b2_all = every_row[:, 0:OUT]
         edge_all = every_row[:, OUT : OUT + EDGES]
         added = const.tile([P, ROW_SETS, EDGES], F32)
 
         def prepare_biases():
-            for n in range(OUT // BANK + 1):
-                cols = slice(n * BANK, (n + 1) * BANK)
-                spread = banks.tile([P, BANK], F32, tag="bank")
-                nc.tensor.matmul(out=spread[:], lhsT=ones[:], rhs=one_row[:, cols], start=True, stop=True)
-                nc.scalar.copy(out=every_row[:, cols], in_=spread[:])
+            for start in range(0, OUT + EDGES, 2 * BANK):
+                end = min(start + 2 * BANK, OUT + EDGES)
+                spread = banks.tile([P, 2 * BANK], BF16, tag="bank")
+                for n in range(start, end, BANK):
+                    stop = min(n + BANK, end)
+                    nc.tensor.matmul(
+                        out=spread[:, n - start : stop - start], lhsT=ones[:], rhs=one_row[:, n:stop], start=True, stop=True
+                    )
+                nc.vector.tensor_copy(out=every_row[:, start:end], in_=spread[:, 0 : end - start])
             b1_f32 = const.tile([P, ROW_SETS], F32)
             nc.vector.tensor_copy(out=b1_f32[:], in_=b1_bf[:])
             w1_edge = const.tile([P, ROW_SETS], F32)
@@ -155,48 +210,61 @@ def tile_edgenetwork_k_kernel(
 
         x_codes = []
         x_scales = []
-        for kq in range(ROW_UNITS):
-            x_unit_codes = const.tile([P, K_UNIT // PACK], U32, name="x_codes%d" % kq, align_bytes=64)
-            x_unit_scales = const.tile([P, K_UNIT // PACK], U8, name="x_scales%d" % kq, align_bytes=64)
-            quantise_unit(x_banks[kq * UNIT_BANKS : (kq + 1) * UNIT_BANKS], x_unit_codes, x_unit_scales)
-            x_codes.append(x_unit_codes)
-            x_scales.append(x_unit_scales)
-            if kq == 0:
+        for i in range(X_PIECES):
+            piece_codes = const.tile([P, X_PIECE_PASSES * P], U32, name="x_codes%d" % i, align_bytes=64)
+            piece_scales = const.tile([P, X_PIECE_PASSES * P], U8, name="x_scales%d" % i, align_bytes=64)
+            quantise_banks(x_reads[i * X_BANKS : (i + 1) * X_BANKS], (0,) if i % 2 else (), piece_codes, piece_scales)
+            x_codes.append(piece_codes)
+            x_scales.append(piece_scales)
+            if i == BIAS_PIECE:
                 prepare_biases()
+            if i >= X_PIECES - ORDER_LEAD:
+                order_next_unit()
 
-        pre = sums.tile([P, ROW_SETS, EDGES], F32)
+        pre_first = sums.tile([P, LAST, EDGES], F32)
+        pre_last = sums.tile([P, 1, EDGES], F32)
         h_grouped = const.tile([P, EDGES, PACK], BF16, align_bytes=64)
 
-        def multiply_unit(u, w_codes, w_scales):
-            t, kq = divmod(u, ROW_UNITS)
-            for i in range(UNIT_PASSES):
-                cols = slice(i * P, (i + 1) * P)
+        def hidden(pre, t0, t1):
+            h_f32 = results.tile([P, t1 - t0, EDGES], F32)
+            nc.vector.tensor_tensor(out=h_f32[:], in0=pre[:], in1=added[:, t0:t1, :], op=ADD)
+            nc.scalar.activation(
+                out=h_grouped[:, :, t0:t1], in_=h_f32[:].rearrange("p t e -> p e t"), func=RELU
+            )
+
+        def multiply_unit(unit, w_codes, w_scales):
+            t, first, size = unit
+            pre = pre_last[:, 0, :] if t == LAST else pre_first[:, t, :]
+            for i in range(size * BANK_PASSES):
+                k_pass = first * BANK_PASSES + i
+                piece, i_x = divmod(k_pass, X_PIECE_PASSES)
+                w_cols = slice(i * P, (i + 1) * P)
+                x_cols = slice(i_x * P, (i_x + 1) * P)
                 nc.tensor.matmul_mx(
-                    out=pre[:, t, :],
-                    lhsT=w_codes[:, cols].bitcast(FP8X4),
-                    lhsT_scale=w_scales[:, cols],
-                    rhs=x_codes[kq][:, cols].bitcast(FP8X4),
-                    rhs_scale=x_scales[kq][:, cols],
-                    start=(kq == 0 and i == 0),
-                    stop=(kq == ROW_UNITS - 1 and i == UNIT_PASSES - 1),
+                    out=pre,
+                    lhsT=w_codes[:, w_cols].bitcast(FP8X4),
+                    lhsT_scale=w_scales[:, w_cols],
+                    rhs=x_codes[piece][:, x_cols].bitcast(FP8X4),
+                    rhs_scale=x_scales[piece][:, x_cols],
+                    start=(k_pass == 0),
+                    stop=(k_pass == NODE_K // K_PASS - 1),
                 )
-            if kq == ROW_UNITS - 1:
-                h_f32 = results.tile([P, EDGES], F32)
-                nc.vector.tensor_tensor(out=h_f32[:], in0=pre[:, t, :], in1=added[:, t, :], op=ADD)
-                nc.scalar.activation(out=h_grouped[:, :, t], in_=h_f32[:], func=RELU)
 
         quantised = []
-        for u in range(W_UNITS + MX_LAG):
-            if u < W_UNITS:
-                w_codes = codes.tile([P, K_UNIT // PACK], U32, align_bytes=64)
-                w_scales = codes.tile([P, K_UNIT // PACK], U8, align_bytes=64)
-                w_pairs = w_raw[u][:].bitcast(F32)
-                quantise_unit([w_pairs[:, j * BANK : (j + 1) * BANK] for j in range(UNIT_BANKS)], w_codes, w_scales)
+        for u in range(len(units) + MX_LAG):
+            if u < len(units):
+                w_codes = codes.tile([P, UNIT_BANKS * BANK_PASSES * P], U32, align_bytes=64)
+                w_scales = codes.tile([P, UNIT_BANKS * BANK_PASSES * P], U8, align_bytes=64)
+                vector_banks = () if len(w_reads[u]) == UNIT_BANKS else (0,)
+                quantise_banks(w_reads[u], vector_banks, w_codes, w_scales)
+                order_next_unit()
                 quantised.append((w_codes, w_scales))
-            if u + W_BUFS < W_UNITS:
-                load_w_unit(u + W_BUFS)
+            load_next_unit()
             if u >= MX_LAG:
-                multiply_unit(u - MX_LAG, *quantised[u - MX_LAG])
+                multiply_unit(units[u - MX_LAG], *quantised[u - MX_LAG])
+                if u - MX_LAG > 0 and units[u - MX_LAG][0] == LAST and units[u - MX_LAG - 1][0] == LAST - 1:
+                    hidden(pre_first, 0, LAST)
+        hidden(pre_last, LAST, ROW_SETS)
 
         scale_rows = W2_scales[0].rearrange("(q r) n -> r q n", r=4)
         for r in range(4):
@@ -213,11 +281,13 @@ def tile_edgenetwork_k_kernel(
             out=h_codes[:].bitcast(FP8X4), scales=h_scales[:], in_=h_grouped[:].rearrange("p e t -> p (e t)")
         )
 
-        for n in range(OUT // BANK):
-            cols = slice(n * BANK, (n + 1) * BANK)
+        start = 0
+        for width in (BANK, BANK, BANK, BANK // 2, BANK // 2):
+            cols = slice(start, start + width)
+            start += width
             product = banks.tile([P, BANK], F32, tag="bank")
             nc.tensor.matmul_mx(
-                out=product[:],
+                out=product[:, 0:width],
                 lhsT=h_codes[:].bitcast(FP8X4),
                 lhsT_scale=h_scales[:],
                 rhs=w2_codes[:, cols].bitcast(FP8X4),
@@ -226,7 +296,7 @@ def tile_edgenetwork_k_kernel(
                 stop=True,
             )
             biased = results.tile([P, BANK], F32)
-            nc.vector.tensor_tensor(out=biased[:], in0=product[:], in1=b2_all[:, cols], op=ADD)
+            nc.vector.tensor_tensor(out=biased[:, 0:width], in0=product[:, 0:width], in1=b2_all[:, cols], op=ADD)
             y = results.tile([P, BANK], F32)
-            nc.scalar.activation(out=y[:], in_=biased[:], func=TANH)
-            nc.sync.dma_start(out=out[:, cols], in_=y[:])
+            nc.scalar.activation(out=y[:, 0:width], in_=biased[:, 0:width], func=TANH)
+            nc.sync.dma_start(out=out[:, cols], in_=y[:, 0:width])

@@ -11,7 +11,6 @@ U8 = mybir.dt.uint8
 FP8X4 = mybir.dt.float8_e4m3fn_x4
 ADD = mybir.AluOpType.add
 MULT = mybir.AluOpType.mult
-RELU = mybir.ActivationFunctionType.Relu
 TANH = mybir.ActivationFunctionType.Tanh
 
 P = 128
@@ -24,6 +23,7 @@ OUT = 2048
 ROW_SETS = MID // P
 LAST = ROW_SETS - 1
 BANK = 512
+OUT_BLOCKS = (BANK, BANK, BANK, BANK // 2, BANK // 2)
 PSUM_BANKS = 8
 SUM_BANKS = 2
 
@@ -37,9 +37,9 @@ X_PIECES = NODE_K // K_BANK // X_BANKS
 X_PIECE_PASSES = X_BANKS * BANK_PASSES
 BIAS_PIECE = 1
 W_STRIDED = 1
-W_BUFS = 8
-ORDER_LEAD = 2
-MX_LAG = 2
+W_BUFS = 7
+ORDER_LEAD = 3
+MX_LAG = 3
 
 FLOPS = 2 * EDGES * (NODE_K + 1) * MID + 2 * EDGES * MID * OUT
 
@@ -82,7 +82,7 @@ def tile_edgenetwork_k_kernel(
         ordered_pool = stack.enter_context(tc.tile_pool(name="ordered", bufs=ORDER_LEAD + 2))
         grouped_pool = stack.enter_context(tc.tile_pool(name="grouped", bufs=3))
         codes = stack.enter_context(tc.tile_pool(name="codes", bufs=MX_LAG + 2))
-        results = stack.enter_context(tc.tile_pool(name="results", bufs=4))
+        results = stack.enter_context(tc.tile_pool(name="results", bufs=len(OUT_BLOCKS)))
         sums = stack.enter_context(tc.psum_pool(name="sums", bufs=1))
         banks = stack.enter_context(tc.psum_pool(name="banks", bufs=PSUM_BANKS - SUM_BANKS))
         stack.enter_context(tc.manual_schedule())
@@ -113,11 +113,9 @@ def tile_edgenetwork_k_kernel(
         x_reads = []
         for i, part in enumerate(node_inputs):
             x_tile = const.tile([P, part.shape[1]], BF16, name="x_raw%d" % i)
-            first = 0
-            for width in (2 * K_BANK, part.shape[1] - 2 * K_BANK):
-                if width:
-                    nc.sync.dma_start(out=x_tile[:, first : first + width], in_=part[:, first : first + width])
-                    first += width
+            width = K_BANK if i == 0 else 2 * K_BANK
+            for first in range(0, part.shape[1], width):
+                nc.sync.dma_start(out=x_tile[:, first : first + width], in_=part[:, first : first + width])
             if i == 0:
                 nc.sync.dma_start(out=one_row[0:1, 0:OUT], in_=b2.unsqueeze(0))
                 nc.sync.dma_start(out=one_row[0:1, OUT : OUT + EDGES], in_=edge_feat.unsqueeze(0))
@@ -184,16 +182,17 @@ def tile_edgenetwork_k_kernel(
         edge_all = every_row[:, OUT : OUT + EDGES]
         added = const.tile([P, ROW_SETS, EDGES], F32)
 
-        def prepare_biases():
-            for start in range(0, OUT + EDGES, 2 * BANK):
-                end = min(start + 2 * BANK, OUT + EDGES)
-                spread = banks.tile([P, 2 * BANK], BF16, tag="bank")
-                for n in range(start, end, BANK):
-                    stop = min(n + BANK, end)
-                    nc.tensor.matmul(
-                        out=spread[:, n - start : stop - start], lhsT=ones[:], rhs=one_row[:, n:stop], start=True, stop=True
-                    )
-                nc.vector.tensor_copy(out=every_row[:, start:end], in_=spread[:, 0 : end - start])
+        def spread_row(start, end, copy):
+            spread = banks.tile([P, 2 * BANK], BF16, tag="bank")
+            for n in range(start, end, BANK):
+                stop = min(n + BANK, end)
+                nc.tensor.matmul(
+                    out=spread[:, n - start : stop - start], lhsT=ones[:], rhs=one_row[:, n:stop], start=True, stop=True
+                )
+            copy(out=every_row[:, start:end], in_=spread[:, 0 : end - start])
+
+        def prepare_added():
+            spread_row(OUT, OUT + EDGES, nc.vector.tensor_copy)
             b1_f32 = const.tile([P, ROW_SETS], F32)
             nc.vector.tensor_copy(out=b1_f32[:], in_=b1_bf[:])
             w1_edge = const.tile([P, ROW_SETS], F32)
@@ -217,20 +216,16 @@ def tile_edgenetwork_k_kernel(
             x_codes.append(piece_codes)
             x_scales.append(piece_scales)
             if i == BIAS_PIECE:
-                prepare_biases()
+                prepare_added()
             if i >= X_PIECES - ORDER_LEAD:
                 order_next_unit()
 
         pre_first = sums.tile([P, LAST, EDGES], F32)
         pre_last = sums.tile([P, 1, EDGES], F32)
-        h_grouped = const.tile([P, EDGES, PACK], BF16, align_bytes=64)
+        before_relu = const.tile([P, ROW_SETS, EDGES], F32)
 
-        def hidden(pre, t0, t1):
-            h_f32 = results.tile([P, t1 - t0, EDGES], F32)
-            nc.vector.tensor_tensor(out=h_f32[:], in0=pre[:], in1=added[:, t0:t1, :], op=ADD)
-            nc.scalar.activation(
-                out=h_grouped[:, :, t0:t1], in_=h_f32[:].rearrange("p t e -> p e t"), func=RELU
-            )
+        def add_row_sets(pre, t0, t1):
+            nc.vector.tensor_tensor(out=before_relu[:, t0:t1, :], in0=pre[:], in1=added[:, t0:t1, :], op=ADD)
 
         def multiply_unit(unit, w_codes, w_scales):
             t, first, size = unit
@@ -260,11 +255,16 @@ def tile_edgenetwork_k_kernel(
                 order_next_unit()
                 quantised.append((w_codes, w_scales))
             load_next_unit()
+            if u == len(units):
+                for start in range(0, OUT, 2 * BANK):
+                    spread_row(start, start + 2 * BANK, nc.scalar.copy)
             if u >= MX_LAG:
                 multiply_unit(units[u - MX_LAG], *quantised[u - MX_LAG])
                 if u - MX_LAG > 0 and units[u - MX_LAG][0] == LAST and units[u - MX_LAG - 1][0] == LAST - 1:
-                    hidden(pre_first, 0, LAST)
-        hidden(pre_last, LAST, ROW_SETS)
+                    add_row_sets(pre_first, 0, LAST)
+        add_row_sets(pre_last, LAST, ROW_SETS)
+        h_grouped = const.tile([P, EDGES, PACK], BF16, align_bytes=64)
+        nc.vector.tensor_scalar_max(h_grouped[:], before_relu[:].rearrange("p t e -> p e t"), 0.0)
 
         scale_rows = W2_scales[0].rearrange("(q r) n -> r q n", r=4)
         for r in range(4):
@@ -282,7 +282,7 @@ def tile_edgenetwork_k_kernel(
         )
 
         start = 0
-        for width in (BANK, BANK, BANK, BANK // 2, BANK // 2):
+        for width in OUT_BLOCKS:
             cols = slice(start, start + width)
             start += width
             product = banks.tile([P, BANK], F32, tag="bank")

@@ -23,38 +23,24 @@ OUT = 2048
 ROW_SETS = MID // P
 LAST = ROW_SETS - 1
 BANK = 512
-OUT_BLOCKS = (BANK, BANK, BANK, BANK // 2, BANK // 2)
+OUT_BLOCKS = (BANK // 2, BANK, BANK, BANK, BANK // 2)
 PSUM_BANKS = 8
 SUM_BANKS = 2
 
 K_BANK = 2 * BANK
 BANK_PASSES = K_BANK // K_PASS
 READS = 2 * BANK_PASSES
-QUANT_BANKS = 2
-UNIT_BANKS = 4
-X_BANKS = 2
-X_PIECES = NODE_K // K_BANK // X_BANKS
-X_PIECE_PASSES = X_BANKS * BANK_PASSES
+PIECE_BANKS = 2
+PIECE_COLS = PIECE_BANKS * K_BANK
+PIECE_PASSES = PIECE_BANKS * BANK_PASSES
+PIECES = NODE_K // PIECE_COLS
+ROUND = 2
 BIAS_PIECE = 1
-W_STRIDED = 1
-W_BUFS = 7
-ORDER_LEAD = 3
-MX_LAG = 3
+W_BUFS = 14
+ORDER_LEAD = 4
+MX_LAG = 2
 
 FLOPS = 2 * EDGES * (NODE_K + 1) * MID + 2 * EDGES * MID * OUT
-
-
-def w1_units():
-    units = []
-    for t in range(ROW_SETS):
-        sizes = [UNIT_BANKS] * (NODE_K // K_BANK // UNIT_BANKS)
-        if t == LAST:
-            sizes[-1:] = [UNIT_BANKS // 2] * 2
-        first = 0
-        for size in sizes:
-            units.append((t, first, size))
-            first += size
-    return units
 
 
 def tile_edgenetwork_k_kernel(
@@ -74,14 +60,14 @@ def tile_edgenetwork_k_kernel(
     nc = tc.nc
     node_inputs = (dst_node_feat, dst_node_hidden, src_node_feat, src_node_hidden)
     w1_sets = W1.rearrange("(p t) k -> t p k", t=ROW_SETS)
-    units = w1_units()
+    w_pieces = [(t, i) for t in range(ROW_SETS) for i in range(PIECES)]
 
     with ExitStack() as stack:
         const = stack.enter_context(tc.tile_pool(name="const", bufs=1))
         raw = stack.enter_context(tc.tile_pool(name="raw", bufs=W_BUFS))
-        ordered_pool = stack.enter_context(tc.tile_pool(name="ordered", bufs=ORDER_LEAD + 2))
-        grouped_pool = stack.enter_context(tc.tile_pool(name="grouped", bufs=3))
-        codes = stack.enter_context(tc.tile_pool(name="codes", bufs=MX_LAG + 2))
+        ordered_pool = stack.enter_context(tc.tile_pool(name="ordered", bufs=ORDER_LEAD + 2 * ROUND))
+        grouped_pool = stack.enter_context(tc.tile_pool(name="grouped", bufs=3 * ROUND))
+        codes = stack.enter_context(tc.tile_pool(name="codes", bufs=(MX_LAG + 2) * ROUND))
         results = stack.enter_context(tc.tile_pool(name="results", bufs=len(OUT_BLOCKS)))
         sums = stack.enter_context(tc.psum_pool(name="sums", bufs=1))
         banks = stack.enter_context(tc.psum_pool(name="banks", bufs=PSUM_BANKS - SUM_BANKS))
@@ -124,58 +110,49 @@ def tile_edgenetwork_k_kernel(
 
         w_raw = []
 
-        def load_next_unit():
-            if len(w_raw) < len(units):
-                t, first, size = units[len(w_raw)]
-                w_tile = raw.tile([P, UNIT_BANKS * K_BANK], BF16)
-                nc.sync.dma_start(
-                    out=w_tile[:, 0 : size * K_BANK], in_=w1_sets[t][:, first * K_BANK : (first + size) * K_BANK]
-                )
+        def load_next_piece():
+            if len(w_raw) < len(w_pieces):
+                t, i = w_pieces[len(w_raw)]
+                w_tile = raw.tile([P, PIECE_COLS], BF16)
+                nc.sync.dma_start(out=w_tile[:], in_=w1_sets[t][:, i * PIECE_COLS : (i + 1) * PIECE_COLS])
                 w_raw.append(w_tile[:].bitcast(F32))
 
-        for u in range(W_BUFS):
-            load_next_unit()
+        for n in range(W_BUFS):
+            load_next_piece()
 
         w_reads = []
 
-        def order_next_unit():
-            if len(w_reads) < len(units):
-                size = units[len(w_reads)][2]
-                pairs = w_raw[len(w_reads)]
-                strided = W_STRIDED if size == UNIT_BANKS else size
+        def order_next_piece():
+            n = len(w_reads)
+            if n < len(w_pieces):
+                pairs = w_raw[n]
+                strided = 1 if n % ROUND == ROUND - 1 else 0
                 reads = [strided_reads(pairs[:, j * BANK : (j + 1) * BANK]) for j in range(strided)]
-                if strided < size:
-                    ordered = ordered_pool.tile([P, (UNIT_BANKS - W_STRIDED) * BANK], F32)
-                    nc.vector.tensor_copy(
-                        out=ordered[:].rearrange("p (g u w) -> p g u w", u=2, w=P),
-                        in_=pairs[:, strided * BANK :].rearrange("p (g w u) -> p g u w", u=2, w=P),
-                    )
-                    for j in range(size - strided):
-                        reads.append([ordered[:, (j * READS + b) * P : (j * READS + b + 1) * P] for b in range(READS)])
+                ordered = ordered_pool.tile([P, PIECE_BANKS * BANK], F32)
+                nc.vector.tensor_copy(
+                    out=ordered[:, strided * BANK :].rearrange("p (g u w) -> p g u w", u=2, w=P),
+                    in_=pairs[:, strided * BANK :].rearrange("p (g w u) -> p g u w", u=2, w=P),
+                )
+                for j in range(strided, PIECE_BANKS):
+                    reads.append([ordered[:, (j * READS + b) * P : (j * READS + b + 1) * P] for b in range(READS)])
                 w_reads.append(reads)
 
-        def quantise_banks(bank_reads, vector_banks, to_codes, to_scales):
-            size = len(bank_reads)
-            grouped = grouped_pool.tile([P, UNIT_BANKS * K_BANK], BF16, align_bytes=64)
+        def group_piece(bank_reads):
+            grouped = grouped_pool.tile([P, PIECE_COLS], BF16, align_bytes=64)
             for j, reads in enumerate(bank_reads):
                 bank = banks.tile([P, READS, P], F32, tag="bank")
                 for b, read in enumerate(reads):
                     nc.tensor.transpose(bank[:, b, :], read, ident[:])
-                copy = nc.vector.tensor_copy if j in vector_banks else nc.scalar.copy
-                copy(
+                nc.scalar.copy(
                     out=grouped[:].bitcast(F32)[:, j * BANK : (j + 1) * BANK].rearrange(
                         "p (g r u) -> p g r u", g=BANK_PASSES, u=2
                     ),
                     in_=bank[:].rearrange("p (g u) r -> p g r u", u=2),
                 )
-            for j in range(0, size, QUANT_BANKS):
-                end = min(j + QUANT_BANKS, size)
-                words = slice(j * BANK_PASSES * P, end * BANK_PASSES * P)
-                nc.vector.quantize_mx(
-                    out=to_codes[:, words].bitcast(FP8X4),
-                    scales=to_scales[:, words],
-                    in_=grouped[:, j * K_BANK : end * K_BANK],
-                )
+            return grouped
+
+        def quantise_piece(grouped, to_codes, to_scales):
+            nc.vector.quantize_mx(out=to_codes[:].bitcast(FP8X4), scales=to_scales[:], in_=grouped[:])
 
         every_row = const.tile([P, OUT + EDGES], BF16)
         b2_all = every_row[:, 0:OUT]
@@ -209,16 +186,18 @@ def tile_edgenetwork_k_kernel(
 
         x_codes = []
         x_scales = []
-        for i in range(X_PIECES):
-            piece_codes = const.tile([P, X_PIECE_PASSES * P], U32, name="x_codes%d" % i, align_bytes=64)
-            piece_scales = const.tile([P, X_PIECE_PASSES * P], U8, name="x_scales%d" % i, align_bytes=64)
-            quantise_banks(x_reads[i * X_BANKS : (i + 1) * X_BANKS], (0,) if i % 2 else (), piece_codes, piece_scales)
+        for i in range(PIECES):
+            piece_codes = const.tile([P, PIECE_PASSES * P], U32, name="x_codes%d" % i, align_bytes=64)
+            piece_scales = const.tile([P, PIECE_PASSES * P], U8, name="x_scales%d" % i, align_bytes=64)
+            grouped = group_piece(x_reads[i * PIECE_BANKS : (i + 1) * PIECE_BANKS])
+            quantise_piece(grouped, piece_codes, piece_scales)
             x_codes.append(piece_codes)
             x_scales.append(piece_scales)
             if i == BIAS_PIECE:
                 prepare_added()
-            if i >= X_PIECES - ORDER_LEAD:
-                order_next_unit()
+            if i >= PIECES - 2:
+                for n in range(ORDER_LEAD // 2):
+                    order_next_piece()
 
         pre_first = sums.tile([P, LAST, EDGES], F32)
         pre_last = sums.tile([P, 1, EDGES], F32)
@@ -227,41 +206,39 @@ def tile_edgenetwork_k_kernel(
         def add_row_sets(pre, t0, t1):
             nc.vector.tensor_tensor(out=before_relu[:, t0:t1, :], in0=pre[:], in1=added[:, t0:t1, :], op=ADD)
 
-        def multiply_unit(unit, w_codes, w_scales):
-            t, first, size = unit
-            pre = pre_last[:, 0, :] if t == LAST else pre_first[:, t, :]
-            for i in range(size * BANK_PASSES):
-                k_pass = first * BANK_PASSES + i
-                piece, i_x = divmod(k_pass, X_PIECE_PASSES)
-                w_cols = slice(i * P, (i + 1) * P)
-                x_cols = slice(i_x * P, (i_x + 1) * P)
+        def multiply_piece(n):
+            t, i = w_pieces[n]
+            w_codes, w_scales = quantised[n]
+            for j in range(PIECE_PASSES):
+                cols = slice(j * P, (j + 1) * P)
                 nc.tensor.matmul_mx(
-                    out=pre,
-                    lhsT=w_codes[:, w_cols].bitcast(FP8X4),
-                    lhsT_scale=w_scales[:, w_cols],
-                    rhs=x_codes[piece][:, x_cols].bitcast(FP8X4),
-                    rhs_scale=x_scales[piece][:, x_cols],
-                    start=(k_pass == 0),
-                    stop=(k_pass == NODE_K // K_PASS - 1),
+                    out=pre_last[:, 0, :] if t == LAST else pre_first[:, t, :],
+                    lhsT=w_codes[:, cols].bitcast(FP8X4),
+                    lhsT_scale=w_scales[:, cols],
+                    rhs=x_codes[i][:, cols].bitcast(FP8X4),
+                    rhs_scale=x_scales[i][:, cols],
+                    start=(i == 0 and j == 0),
+                    stop=(i == PIECES - 1 and j == PIECE_PASSES - 1),
                 )
 
         quantised = []
-        for u in range(len(units) + MX_LAG):
-            if u < len(units):
-                w_codes = codes.tile([P, UNIT_BANKS * BANK_PASSES * P], U32, align_bytes=64)
-                w_scales = codes.tile([P, UNIT_BANKS * BANK_PASSES * P], U8, align_bytes=64)
-                vector_banks = () if len(w_reads[u]) == UNIT_BANKS else (0,)
-                quantise_banks(w_reads[u], vector_banks, w_codes, w_scales)
-                order_next_unit()
-                quantised.append((w_codes, w_scales))
-            load_next_unit()
-            if u == len(units):
+        rounds = len(w_pieces) // ROUND
+        for r in range(rounds + MX_LAG):
+            if r < rounds:
+                for n in range(r * ROUND, (r + 1) * ROUND):
+                    w_codes = codes.tile([P, PIECE_PASSES * P], U32, align_bytes=64)
+                    w_scales = codes.tile([P, PIECE_PASSES * P], U8, align_bytes=64)
+                    quantise_piece(group_piece(w_reads[n]), w_codes, w_scales)
+                    quantised.append((w_codes, w_scales))
+                    order_next_piece()
+                    load_next_piece()
+            if r == rounds:
                 for start in range(0, OUT, 2 * BANK):
                     spread_row(start, start + 2 * BANK, nc.scalar.copy)
-            if u >= MX_LAG:
-                multiply_unit(units[u - MX_LAG], *quantised[u - MX_LAG])
-                if u - MX_LAG > 0 and units[u - MX_LAG][0] == LAST and units[u - MX_LAG - 1][0] == LAST - 1:
-                    add_row_sets(pre_first, 0, LAST)
+            if r >= MX_LAG:
+                for n in range((r - MX_LAG) * ROUND, (r - MX_LAG + 1) * ROUND):
+                    multiply_piece(n)
+        add_row_sets(pre_first, 0, LAST)
         add_row_sets(pre_last, LAST, ROW_SETS)
         h_grouped = const.tile([P, EDGES, PACK], BF16, align_bytes=64)
         nc.vector.tensor_scalar_max(h_grouped[:], before_relu[:].rearrange("p t e -> p e t"), 0.0)

@@ -23,7 +23,7 @@ OUT = 2048
 ROW_SETS = MID // P
 LAST = ROW_SETS - 1
 BANK = 512
-OUT_BLOCKS = (BANK // 2, BANK, BANK, BANK, BANK // 2)
+OUT_BLOCK = 256
 PSUM_BANKS = 8
 SUM_BANKS = 2
 
@@ -34,9 +34,10 @@ PIECE_BANKS = 2
 PIECE_COLS = PIECE_BANKS * K_BANK
 PIECE_PASSES = PIECE_BANKS * BANK_PASSES
 PIECES = NODE_K // PIECE_COLS
+X_LOADS = (((0, 1024), (1024, 2048)), ((0, 2048), (2048, 6144)), ((0, 2048),), ((0, 4096), (4096, 6144)))
 ROUND = 2
 BIAS_PIECE = 1
-W_BUFS = 14
+W_BUFS = 7
 ORDER_LEAD = 4
 MX_LAG = 2
 
@@ -61,6 +62,7 @@ def tile_edgenetwork_k_kernel(
     node_inputs = (dst_node_feat, dst_node_hidden, src_node_feat, src_node_hidden)
     w1_sets = W1.rearrange("(p t) k -> t p k", t=ROW_SETS)
     w_pieces = [(t, i) for t in range(ROW_SETS) for i in range(PIECES)]
+    rounds = len(w_pieces) // ROUND
 
     with ExitStack() as stack:
         const = stack.enter_context(tc.tile_pool(name="const", bufs=1))
@@ -68,7 +70,7 @@ def tile_edgenetwork_k_kernel(
         ordered_pool = stack.enter_context(tc.tile_pool(name="ordered", bufs=ORDER_LEAD + 2 * ROUND))
         grouped_pool = stack.enter_context(tc.tile_pool(name="grouped", bufs=3 * ROUND))
         codes = stack.enter_context(tc.tile_pool(name="codes", bufs=(MX_LAG + 2) * ROUND))
-        results = stack.enter_context(tc.tile_pool(name="results", bufs=len(OUT_BLOCKS)))
+        results = stack.enter_context(tc.tile_pool(name="results", bufs=OUT // OUT_BLOCK))
         sums = stack.enter_context(tc.psum_pool(name="sums", bufs=1))
         banks = stack.enter_context(tc.psum_pool(name="banks", bufs=PSUM_BANKS - SUM_BANKS))
         stack.enter_context(tc.manual_schedule())
@@ -99,33 +101,39 @@ def tile_edgenetwork_k_kernel(
         x_reads = []
         for i, part in enumerate(node_inputs):
             x_tile = const.tile([P, part.shape[1]], BF16, name="x_raw%d" % i)
-            width = K_BANK if i == 0 else 2 * K_BANK
-            for first in range(0, part.shape[1], width):
-                nc.sync.dma_start(out=x_tile[:, first : first + width], in_=part[:, first : first + width])
+            for first, end in X_LOADS[i]:
+                nc.sync.dma_start(out=x_tile[:, first:end], in_=part[:, first:end])
             if i == 0:
                 nc.sync.dma_start(out=one_row[0:1, 0:OUT], in_=b2.unsqueeze(0))
                 nc.sync.dma_start(out=one_row[0:1, OUT : OUT + EDGES], in_=edge_feat.unsqueeze(0))
             for j in range(part.shape[1] // K_BANK):
                 x_reads.append(strided_reads(x_tile[:].bitcast(F32)[:, j * BANK : (j + 1) * BANK]))
 
-        w_raw = []
+        w_pairs = []
 
-        def load_next_piece():
-            if len(w_raw) < len(w_pieces):
-                t, i = w_pieces[len(w_raw)]
-                w_tile = raw.tile([P, PIECE_COLS], BF16)
-                nc.sync.dma_start(out=w_tile[:], in_=w1_sets[t][:, i * PIECE_COLS : (i + 1) * PIECE_COLS])
-                w_raw.append(w_tile[:].bitcast(F32))
+        def load_next_round():
+            n = len(w_pairs)
+            if n < len(w_pieces):
+                w_tile = raw.tile([P, ROUND * PIECE_COLS], BF16)
+                t, i = w_pieces[n]
+                step = ROUND if n + ROUND < len(w_pieces) else 1
+                for j in range(0, ROUND, step):
+                    nc.sync.dma_start(
+                        out=w_tile[:, j * PIECE_COLS : (j + step) * PIECE_COLS],
+                        in_=w1_sets[t][:, (i + j) * PIECE_COLS : (i + j + step) * PIECE_COLS],
+                    )
+                for j in range(ROUND):
+                    w_pairs.append(w_tile[:].bitcast(F32)[:, j * PIECE_BANKS * BANK : (j + 1) * PIECE_BANKS * BANK])
 
-        for n in range(W_BUFS):
-            load_next_piece()
+        for r in range(W_BUFS):
+            load_next_round()
 
         w_reads = []
 
         def order_next_piece():
             n = len(w_reads)
             if n < len(w_pieces):
-                pairs = w_raw[n]
+                pairs = w_pairs[n]
                 strided = 1 if n % ROUND == ROUND - 1 else 0
                 reads = [strided_reads(pairs[:, j * BANK : (j + 1) * BANK]) for j in range(strided)]
                 ordered = ordered_pool.tile([P, PIECE_BANKS * BANK], F32)
@@ -137,13 +145,14 @@ def tile_edgenetwork_k_kernel(
                     reads.append([ordered[:, (j * READS + b) * P : (j * READS + b + 1) * P] for b in range(READS)])
                 w_reads.append(reads)
 
-        def group_piece(bank_reads):
+        def group_piece(bank_reads, vector_banks=()):
             grouped = grouped_pool.tile([P, PIECE_COLS], BF16, align_bytes=64)
             for j, reads in enumerate(bank_reads):
                 bank = banks.tile([P, READS, P], F32, tag="bank")
                 for b, read in enumerate(reads):
                     nc.tensor.transpose(bank[:, b, :], read, ident[:])
-                nc.scalar.copy(
+                copy = nc.vector.tensor_copy if j in vector_banks else nc.scalar.copy
+                copy(
                     out=grouped[:].bitcast(F32)[:, j * BANK : (j + 1) * BANK].rearrange(
                         "p (g r u) -> p g r u", g=BANK_PASSES, u=2
                     ),
@@ -151,8 +160,14 @@ def tile_edgenetwork_k_kernel(
                 )
             return grouped
 
-        def quantise_piece(grouped, to_codes, to_scales):
-            nc.vector.quantize_mx(out=to_codes[:].bitcast(FP8X4), scales=to_scales[:], in_=grouped[:])
+        def quantise_piece(grouped, to_codes, to_scales, calls=1):
+            for c in range(calls):
+                words = slice(c * PIECE_PASSES // calls * P, (c + 1) * PIECE_PASSES // calls * P)
+                nc.vector.quantize_mx(
+                    out=to_codes[:, words].bitcast(FP8X4),
+                    scales=to_scales[:, words],
+                    in_=grouped[:, PACK * words.start : PACK * words.stop],
+                )
 
         every_row = const.tile([P, OUT + EDGES], BF16)
         b2_all = every_row[:, 0:OUT]
@@ -222,22 +237,24 @@ def tile_edgenetwork_k_kernel(
                 )
 
         quantised = []
-        rounds = len(w_pieces) // ROUND
         for r in range(rounds + MX_LAG):
             if r < rounds:
+                grouped_round = []
+                for n in range(r * ROUND, (r + 1) * ROUND):
+                    grouped_round.append(group_piece(w_reads[n], (0,) if n == len(w_pieces) - 1 else ()))
                 for n in range(r * ROUND, (r + 1) * ROUND):
                     w_codes = codes.tile([P, PIECE_PASSES * P], U32, align_bytes=64)
                     w_scales = codes.tile([P, PIECE_PASSES * P], U8, align_bytes=64)
-                    quantise_piece(group_piece(w_reads[n]), w_codes, w_scales)
+                    calls = PIECE_BANKS if n == len(w_pieces) - 1 else 1
+                    quantise_piece(grouped_round[n - r * ROUND], w_codes, w_scales, calls)
                     quantised.append((w_codes, w_scales))
                     order_next_piece()
-                    load_next_piece()
-            if r == rounds:
-                for start in range(0, OUT, 2 * BANK):
-                    spread_row(start, start + 2 * BANK, nc.scalar.copy)
+                load_next_round()
             if r >= MX_LAG:
                 for n in range((r - MX_LAG) * ROUND, (r - MX_LAG + 1) * ROUND):
                     multiply_piece(n)
+        for start in range(0, OUT, BANK):
+            spread_row(start, start + BANK, nc.scalar.copy)
         add_row_sets(pre_first, 0, LAST)
         add_row_sets(pre_last, LAST, ROW_SETS)
         h_grouped = const.tile([P, EDGES, PACK], BF16, align_bytes=64)
@@ -258,13 +275,11 @@ def tile_edgenetwork_k_kernel(
             out=h_codes[:].bitcast(FP8X4), scales=h_scales[:], in_=h_grouped[:].rearrange("p e t -> p (e t)")
         )
 
-        start = 0
-        for width in OUT_BLOCKS:
-            cols = slice(start, start + width)
-            start += width
-            product = banks.tile([P, BANK], F32, tag="bank")
+        for start in range(0, OUT, OUT_BLOCK):
+            cols = slice(start, start + OUT_BLOCK)
+            product = banks.tile([P, OUT_BLOCK], F32, tag="bank")
             nc.tensor.matmul_mx(
-                out=product[:, 0:width],
+                out=product[:],
                 lhsT=h_codes[:].bitcast(FP8X4),
                 lhsT_scale=h_scales[:],
                 rhs=w2_codes[:, cols].bitcast(FP8X4),
@@ -272,8 +287,8 @@ def tile_edgenetwork_k_kernel(
                 start=True,
                 stop=True,
             )
-            biased = results.tile([P, BANK], F32)
-            nc.vector.tensor_tensor(out=biased[:, 0:width], in0=product[:, 0:width], in1=b2_all[:, cols], op=ADD)
-            y = results.tile([P, BANK], F32)
-            nc.scalar.activation(out=y[:, 0:width], in_=biased[:, 0:width], func=TANH)
-            nc.sync.dma_start(out=out[:, cols], in_=y[:, 0:width])
+            biased = results.tile([P, OUT_BLOCK], F32)
+            nc.vector.tensor_tensor(out=biased[:], in0=product[:], in1=b2_all[:, cols], op=ADD)
+            y = results.tile([P, OUT_BLOCK], F32)
+            nc.scalar.activation(out=y[:], in_=biased[:], func=TANH)
+            nc.sync.dma_start(out=out[:, cols], in_=y[:])

@@ -34,7 +34,6 @@ PIECE_BANKS = 2
 PIECE_COLS = PIECE_BANKS * K_BANK
 PIECE_PASSES = PIECE_BANKS * BANK_PASSES
 PIECES = NODE_K // PIECE_COLS
-X_LOADS = (((0, 1024), (1024, 2048)), ((0, 2048), (2048, 6144)), ((0, 2048),), ((0, 4096), (4096, 6144)))
 ROUND = 2
 BIAS_PIECE = 1
 W_BUFS = 7
@@ -94,6 +93,8 @@ def tile_edgenetwork_k_kernel(
                 out=w1_edge_bf[:], in_=W1.rearrange("(p t) k -> p t k", t=ROW_SETS)[:, :, NODE_K : NODE_K + 1]
             )
         nc.scalar.activation(out=warm[:], in_=warm[:], func=TANH)
+        nc.scalar.dma_start(out=one_row[0:1, OUT : OUT + EDGES], in_=edge_feat.unsqueeze(0))
+        nc.scalar.dma_start(out=one_row[0:1, 0:OUT], in_=b2.unsqueeze(0))
 
         def strided_reads(pairs):
             return [pairs[:, 2 * P * g + u : 2 * P * (g + 1) : 2] for g in range(BANK_PASSES) for u in range(2)]
@@ -101,11 +102,7 @@ def tile_edgenetwork_k_kernel(
         x_reads = []
         for i, part in enumerate(node_inputs):
             x_tile = const.tile([P, part.shape[1]], BF16, name="x_raw%d" % i)
-            for first, end in X_LOADS[i]:
-                nc.sync.dma_start(out=x_tile[:, first:end], in_=part[:, first:end])
-            if i == 0:
-                nc.sync.dma_start(out=one_row[0:1, 0:OUT], in_=b2.unsqueeze(0))
-                nc.sync.dma_start(out=one_row[0:1, OUT : OUT + EDGES], in_=edge_feat.unsqueeze(0))
+            nc.sync.dma_start(out=x_tile[:], in_=part)
             for j in range(part.shape[1] // K_BANK):
                 x_reads.append(strided_reads(x_tile[:].bitcast(F32)[:, j * BANK : (j + 1) * BANK]))
 
@@ -210,9 +207,8 @@ def tile_edgenetwork_k_kernel(
             x_scales.append(piece_scales)
             if i == BIAS_PIECE:
                 prepare_added()
-            if i >= PIECES - 2:
-                for n in range(ORDER_LEAD // 2):
-                    order_next_piece()
+            if i >= PIECES - ORDER_LEAD:
+                order_next_piece()
 
         pre_first = sums.tile([P, LAST, EDGES], F32)
         pre_last = sums.tile([P, 1, EDGES], F32)
@@ -264,10 +260,7 @@ def tile_edgenetwork_k_kernel(
         for r in range(4):
             nc.sync.dma_start(out=w2_scales[r:P:32, :].bitcast(I32), in_=scale_rows[r].bitcast(I32))
         w2_codes = const.tile([P, OUT], U32, align_bytes=64)
-        w2_words = W2_words[0].rearrange("p n t -> p (n t)").bitcast(I32)
-        for n in range(OUT // BANK):
-            cols = slice(n * BANK, (n + 1) * BANK)
-            nc.sync.dma_start(out=w2_codes[:, cols].bitcast(I32), in_=w2_words[:, cols])
+        nc.sync.dma_start(out=w2_codes[:].bitcast(I32), in_=W2_words[0].rearrange("p n t -> p (n t)").bitcast(I32))
 
         h_codes = const.tile([P, EDGES], U32, align_bytes=64)
         h_scales = const.tile([P, EDGES], U8, align_bytes=64)

@@ -24,6 +24,7 @@ ROW_SETS = MID // P
 LAST = ROW_SETS - 1
 BANK = 512
 OUT_BLOCK = 256
+STORE = 512
 PSUM_BANKS = 8
 SUM_BANKS = 2
 
@@ -34,8 +35,8 @@ PIECE_BANKS = 2
 PIECE_COLS = PIECE_BANKS * K_BANK
 PIECE_PASSES = PIECE_BANKS * BANK_PASSES
 PIECES = NODE_K // PIECE_COLS
+BIAS_PIECE = 3
 ROUND = 2
-BIAS_PIECE = 1
 W_BUFS = 7
 ORDER_LEAD = 4
 MX_LAG = 2
@@ -93,8 +94,6 @@ def tile_edgenetwork_k_kernel(
                 out=w1_edge_bf[:], in_=W1.rearrange("(p t) k -> p t k", t=ROW_SETS)[:, :, NODE_K : NODE_K + 1]
             )
         nc.scalar.activation(out=warm[:], in_=warm[:], func=TANH)
-        nc.scalar.dma_start(out=one_row[0:1, OUT : OUT + EDGES], in_=edge_feat.unsqueeze(0))
-        nc.scalar.dma_start(out=one_row[0:1, 0:OUT], in_=b2.unsqueeze(0))
 
         def strided_reads(pairs):
             return [pairs[:, 2 * P * g + u : 2 * P * (g + 1) : 2] for g in range(BANK_PASSES) for u in range(2)]
@@ -103,6 +102,9 @@ def tile_edgenetwork_k_kernel(
         for i, part in enumerate(node_inputs):
             x_tile = const.tile([P, part.shape[1]], BF16, name="x_raw%d" % i)
             nc.sync.dma_start(out=x_tile[:], in_=part)
+            if i == 1:
+                nc.sync.dma_start(out=one_row[0:1, 0:OUT], in_=b2.unsqueeze(0))
+                nc.sync.dma_start(out=one_row[0:1, OUT : OUT + EDGES], in_=edge_feat.unsqueeze(0))
             for j in range(part.shape[1] // K_BANK):
                 x_reads.append(strided_reads(x_tile[:].bitcast(F32)[:, j * BANK : (j + 1) * BANK]))
 
@@ -171,17 +173,16 @@ def tile_edgenetwork_k_kernel(
         edge_all = every_row[:, OUT : OUT + EDGES]
         added = const.tile([P, ROW_SETS, EDGES], F32)
 
-        def spread_row(start, end, copy):
-            spread = banks.tile([P, 2 * BANK], BF16, tag="bank")
-            for n in range(start, end, BANK):
-                stop = min(n + BANK, end)
-                nc.tensor.matmul(
-                    out=spread[:, n - start : stop - start], lhsT=ones[:], rhs=one_row[:, n:stop], start=True, stop=True
-                )
-            copy(out=every_row[:, start:end], in_=spread[:, 0 : end - start])
-
-        def prepare_added():
-            spread_row(OUT, OUT + EDGES, nc.vector.tensor_copy)
+        def prepare_biases():
+            for start in range(0, OUT + EDGES, 2 * BANK):
+                end = min(start + 2 * BANK, OUT + EDGES)
+                spread = banks.tile([P, 2 * BANK], BF16, tag="bank")
+                for n in range(start, end, BANK):
+                    stop = min(n + BANK, end)
+                    nc.tensor.matmul(
+                        out=spread[:, n - start : stop - start], lhsT=ones[:], rhs=one_row[:, n:stop], start=True, stop=True
+                    )
+                nc.vector.tensor_copy(out=every_row[:, start:end], in_=spread[:, 0 : end - start])
             b1_f32 = const.tile([P, ROW_SETS], F32)
             nc.vector.tensor_copy(out=b1_f32[:], in_=b1_bf[:])
             w1_edge = const.tile([P, ROW_SETS], F32)
@@ -206,7 +207,7 @@ def tile_edgenetwork_k_kernel(
             x_codes.append(piece_codes)
             x_scales.append(piece_scales)
             if i == BIAS_PIECE:
-                prepare_added()
+                prepare_biases()
             if i >= PIECES - ORDER_LEAD:
                 order_next_piece()
 
@@ -249,8 +250,6 @@ def tile_edgenetwork_k_kernel(
             if r >= MX_LAG:
                 for n in range((r - MX_LAG) * ROUND, (r - MX_LAG + 1) * ROUND):
                     multiply_piece(n)
-        for start in range(0, OUT, BANK):
-            spread_row(start, start + BANK, nc.scalar.copy)
         add_row_sets(pre_first, 0, LAST)
         add_row_sets(pre_last, LAST, ROW_SETS)
         h_grouped = const.tile([P, EDGES, PACK], BF16, align_bytes=64)
@@ -268,6 +267,7 @@ def tile_edgenetwork_k_kernel(
             out=h_codes[:].bitcast(FP8X4), scales=h_scales[:], in_=h_grouped[:].rearrange("p e t -> p (e t)")
         )
 
+        y = const.tile([P, OUT], F32)
         for start in range(0, OUT, OUT_BLOCK):
             cols = slice(start, start + OUT_BLOCK)
             product = banks.tile([P, OUT_BLOCK], F32, tag="bank")
@@ -282,6 +282,7 @@ def tile_edgenetwork_k_kernel(
             )
             biased = results.tile([P, OUT_BLOCK], F32)
             nc.vector.tensor_tensor(out=biased[:], in0=product[:], in1=b2_all[:, cols], op=ADD)
-            y = results.tile([P, OUT_BLOCK], F32)
-            nc.scalar.activation(out=y[:], in_=biased[:], func=TANH)
-            nc.sync.dma_start(out=out[:, cols], in_=y[:])
+            nc.scalar.activation(out=y[:, cols], in_=biased[:], func=TANH)
+            end = start + OUT_BLOCK
+            if end % STORE == 0:
+                nc.sync.dma_start(out=out[:, end - STORE : end], in_=y[:, end - STORE : end])

@@ -88,11 +88,6 @@ def tile_edgenetwork_k_kernel(
 
         b1_bf = const.tile([P, ROW_SETS], BF16)
         nc.scalar.dma_start(out=b1_bf[:], in_=b1.rearrange("(p t) -> p t", t=ROW_SETS))
-        w1_edge_bf = const.tile([P, ROW_SETS, 1], BF16)
-        with nc.allow_non_contiguous_dma(reason="one column of W1: 512 single elements"):
-            nc.scalar.dma_start(
-                out=w1_edge_bf[:], in_=W1.rearrange("(p t) k -> p t k", t=ROW_SETS)[:, :, NODE_K : NODE_K + 1]
-            )
         nc.scalar.activation(out=warm[:], in_=warm[:], func=TANH)
 
         def strided_reads(pairs):
@@ -109,18 +104,23 @@ def tile_edgenetwork_k_kernel(
                 x_reads.append(strided_reads(x_tile[:].bitcast(F32)[:, j * BANK : (j + 1) * BANK]))
 
         w_pairs = []
+        w1_edge = []
 
         def load_next_round():
             n = len(w_pairs)
             if n < len(w_pieces):
-                w_tile = raw.tile([P, ROUND * PIECE_COLS], BF16)
+                w_tile = raw.tile([P, ROUND * PIECE_COLS + 2], BF16)
                 t, i = w_pieces[n]
                 step = ROUND if n + ROUND < len(w_pieces) else 1
                 for j in range(0, ROUND, step):
+                    end = j + step
+                    extra = 1 if i + end == PIECES else 0
                     nc.sync.dma_start(
-                        out=w_tile[:, j * PIECE_COLS : (j + step) * PIECE_COLS],
-                        in_=w1_sets[t][:, (i + j) * PIECE_COLS : (i + j + step) * PIECE_COLS],
+                        out=w_tile[:, j * PIECE_COLS : end * PIECE_COLS + extra],
+                        in_=w1_sets[t][:, (i + j) * PIECE_COLS : (i + end) * PIECE_COLS + extra],
                     )
+                    if extra:
+                        w1_edge.append(w_tile[:, end * PIECE_COLS : end * PIECE_COLS + 1])
                 for j in range(ROUND):
                     w_pairs.append(w_tile[:].bitcast(F32)[:, j * PIECE_BANKS * BANK : (j + 1) * PIECE_BANKS * BANK])
 
@@ -183,19 +183,15 @@ def tile_edgenetwork_k_kernel(
                         out=spread[:, n - start : stop - start], lhsT=ones[:], rhs=one_row[:, n:stop], start=True, stop=True
                     )
                 nc.vector.tensor_copy(out=every_row[:, start:end], in_=spread[:, 0 : end - start])
-            b1_f32 = const.tile([P, ROW_SETS], F32)
-            nc.vector.tensor_copy(out=b1_f32[:], in_=b1_bf[:])
-            w1_edge = const.tile([P, ROW_SETS], F32)
-            nc.vector.tensor_copy(out=w1_edge[:], in_=w1_edge_bf[:, :, 0])
-            for t in range(ROW_SETS):
-                nc.vector.tensor_scalar(
-                    out=added[:, t, :],
-                    in0=edge_all,
-                    scalar1=w1_edge[:, t : t + 1],
-                    scalar2=b1_f32[:, t : t + 1],
-                    op0=MULT,
-                    op1=ADD,
-                )
+        def prepare_added(t):
+            nc.vector.tensor_scalar(
+                out=added[:, t, :],
+                in0=edge_all,
+                scalar1=w1_edge[t],
+                scalar2=b1_bf[:, t : t + 1],
+                op0=MULT,
+                op1=ADD,
+            )
 
         x_codes = []
         x_scales = []
@@ -246,10 +242,14 @@ def tile_edgenetwork_k_kernel(
                     quantise_piece(grouped_round[n - r * ROUND], w_codes, w_scales, calls)
                     quantised.append((w_codes, w_scales))
                     order_next_piece()
+                t, i = w_pieces[r * ROUND]
+                if i + ROUND == PIECES and t < LAST:
+                    prepare_added(t)
                 load_next_round()
             if r >= MX_LAG:
                 for n in range((r - MX_LAG) * ROUND, (r - MX_LAG + 1) * ROUND):
                     multiply_piece(n)
+        prepare_added(LAST)
         add_row_sets(pre_first, 0, LAST)
         add_row_sets(pre_last, LAST, ROW_SETS)
         h_grouped = const.tile([P, EDGES, PACK], BF16, align_bytes=64)

from contextlib import ExitStack

import concourse.mybir as mybir
from concourse.masks import make_identity

F32 = mybir.dt.float32
BF16 = mybir.dt.bfloat16
I32 = mybir.dt.int32
U32 = mybir.dt.uint32
U8 = mybir.dt.uint8
FP8X4 = mybir.dt.float8_e4m3fn_x4
ADD = mybir.AluOpType.add
MULT = mybir.AluOpType.mult
TANH = mybir.ActivationFunctionType.Tanh

P = 128
PACK = 4
K_PASS = P * PACK
EDGES = 128
NODE_K = 16384
MID = 512
OUT = 2048
ROW_SETS = MID // P
LAST = ROW_SETS - 1
BANK = 512
OUT_BLOCK = 256
STORE = 512
PSUM_BANKS = 8
SUM_BANKS = 2

K_BANK = 2 * BANK
BANK_PASSES = K_BANK // K_PASS
READS = 2 * BANK_PASSES
PIECE_BANKS = 2
PIECE_COLS = PIECE_BANKS * K_BANK
PIECE_PASSES = PIECE_BANKS * BANK_PASSES
PIECES = NODE_K // PIECE_COLS
BIAS_PIECE = 3
ROUND = 2
W_BUFS = 7
ORDER_LEAD = 4
MX_LAG = 2

FLOPS = 2 * EDGES * (NODE_K + 1) * MID + 2 * EDGES * MID * OUT


def tile_edgenetwork_k_kernel(
    tc,
    dst_node_feat,
    dst_node_hidden,
    src_node_feat,
    src_node_hidden,
    edge_feat,
    W1,
    b1,
    W2_words,
    W2_scales,
    b2,
    out,
):
    nc = tc.nc
    node_inputs = (dst_node_feat, dst_node_hidden, src_node_feat, src_node_hidden)
    w1_sets = W1.rearrange("(p t) k -> t p k", t=ROW_SETS)
    w_pieces = [(t, i) for t in range(ROW_SETS) for i in range(PIECES)]
    rounds = len(w_pieces) // ROUND

    with ExitStack() as stack:
        const = stack.enter_context(tc.tile_pool(name="const", bufs=1))
        raw = stack.enter_context(tc.tile_pool(name="raw", bufs=W_BUFS))
        ordered_pool = stack.enter_context(tc.tile_pool(name="ordered", bufs=ORDER_LEAD + 2 * ROUND))
        grouped_pool = stack.enter_context(tc.tile_pool(name="grouped", bufs=3 * ROUND))
        codes = stack.enter_context(tc.tile_pool(name="codes", bufs=(MX_LAG + 2) * ROUND))
        results = stack.enter_context(tc.tile_pool(name="results", bufs=OUT // OUT_BLOCK))
        sums = stack.enter_context(tc.psum_pool(name="sums", bufs=1))
        banks = stack.enter_context(tc.psum_pool(name="banks", bufs=PSUM_BANKS - SUM_BANKS))
        stack.enter_context(tc.manual_schedule())

        one_row = const.tile([P, OUT + EDGES], BF16)
        nc.vector.memset(one_row[:].bitcast(I32), 0)
        ones = const.tile([P, P], BF16)
        nc.vector.memset(ones[:], 1.0)
        warm = const.tile([P, 1], F32)
        nc.vector.memset(warm[:], 0.0)
        w2_scales = const.tile([P, OUT], U8, align_bytes=64)
        nc.vector.memset(w2_scales[:].bitcast(I32), 0)
        ident = const.tile([P, P], F32)
        make_identity(nc, ident[:])

        b1_bf = const.tile([P, ROW_SETS], BF16)
        nc.scalar.dma_start(out=b1_bf[:], in_=b1.rearrange("(p t) -> p t", t=ROW_SETS))
        nc.scalar.activation(out=warm[:], in_=warm[:], func=TANH)

        def strided_reads(pairs):
            return [pairs[:, 2 * P * g + u : 2 * P * (g + 1) : 2] for g in range(BANK_PASSES) for u in range(2)]

        x_reads = []
        for i, part in enumerate(node_inputs):
            x_tile = const.tile([P, part.shape[1]], BF16, name="x_raw%d" % i)
            nc.sync.dma_start(out=x_tile[:], in_=part)
            if i == 1:
                nc.sync.dma_start(out=one_row[0:1, 0:OUT], in_=b2.unsqueeze(0))
                nc.sync.dma_start(out=one_row[0:1, OUT : OUT + EDGES], in_=edge_feat.unsqueeze(0))
            for j in range(part.shape[1] // K_BANK):
                x_reads.append(strided_reads(x_tile[:].bitcast(F32)[:, j * BANK : (j + 1) * BANK]))

        w_pairs = []
        w1_edge = []

        def load_next_round():
            n = len(w_pairs)
            if n < len(w_pieces):
                w_tile = raw.tile([P, ROUND * PIECE_COLS + 2], BF16)
                t, i = w_pieces[n]
                step = ROUND if n + ROUND < len(w_pieces) else 1
                for j in range(0, ROUND, step):
                    end = j + step
                    extra = 1 if i + end == PIECES else 0
                    nc.sync.dma_start(
                        out=w_tile[:, j * PIECE_COLS : end * PIECE_COLS + extra],
                        in_=w1_sets[t][:, (i + j) * PIECE_COLS : (i + end) * PIECE_COLS + extra],
                    )
                    if extra:
                        w1_edge.append(w_tile[:, end * PIECE_COLS : end * PIECE_COLS + 1])
                for j in range(ROUND):
                    w_pairs.append(w_tile[:].bitcast(F32)[:, j * PIECE_BANKS * BANK : (j + 1) * PIECE_BANKS * BANK])

        for r in range(W_BUFS):
            load_next_round()

        w_reads = []

        def order_next_piece():
            n = len(w_reads)
            if n < len(w_pieces):
                pairs = w_pairs[n]
                strided = 1 if n % ROUND == ROUND - 1 else 0
                reads = [strided_reads(pairs[:, j * BANK : (j + 1) * BANK]) for j in range(strided)]
                ordered = ordered_pool.tile([P, PIECE_BANKS * BANK], F32)
                nc.vector.tensor_copy(
                    out=ordered[:, strided * BANK :].rearrange("p (g u w) -> p g u w", u=2, w=P),
                    in_=pairs[:, strided * BANK :].rearrange("p (g w u) -> p g u w", u=2, w=P),
                )
                for j in range(strided, PIECE_BANKS):
                    reads.append([ordered[:, (j * READS + b) * P : (j * READS + b + 1) * P] for b in range(READS)])
                w_reads.append(reads)

        def group_piece(bank_reads, vector_banks=()):
            grouped = grouped_pool.tile([P, PIECE_COLS], BF16, align_bytes=64)
            for j, reads in enumerate(bank_reads):
                bank = banks.tile([P, READS, P], F32, tag="bank")
                for b, read in enumerate(reads):
                    nc.tensor.transpose(bank[:, b, :], read, ident[:])
                copy = nc.vector.tensor_copy if j in vector_banks else nc.scalar.copy
                copy(
                    out=grouped[:].bitcast(F32)[:, j * BANK : (j + 1) * BANK].rearrange(
                        "p (g r u) -> p g r u", g=BANK_PASSES, u=2
                    ),
                    in_=bank[:].rearrange("p (g u) r -> p g r u", u=2),
                )
            return grouped

        def quantise_piece(grouped, to_codes, to_scales, calls=1):
            for c in range(calls):
                words = slice(c * PIECE_PASSES // calls * P, (c + 1) * PIECE_PASSES // calls * P)
                nc.vector.quantize_mx(
                    out=to_codes[:, words].bitcast(FP8X4),
                    scales=to_scales[:, words],
                    in_=grouped[:, PACK * words.start : PACK * words.stop],
                )

        every_row = const.tile([P, OUT + EDGES], BF16)
        b2_all = every_row[:, 0:OUT]
        edge_all = every_row[:, OUT : OUT + EDGES]
        added = const.tile([P, ROW_SETS, EDGES], F32)

        def prepare_biases():
            for start in range(0, OUT + EDGES, 2 * BANK):
                end = min(start + 2 * BANK, OUT + EDGES)
                spread = banks.tile([P, 2 * BANK], BF16, tag="bank")
                for n in range(start, end, BANK):
                    stop = min(n + BANK, end)
                    nc.tensor.matmul(
                        out=spread[:, n - start : stop - start], lhsT=ones[:], rhs=one_row[:, n:stop], start=True, stop=True
                    )
                nc.vector.tensor_copy(out=every_row[:, start:end], in_=spread[:, 0 : end - start])
        def prepare_added(t):
            nc.vector.tensor_scalar(
                out=added[:, t, :],
                in0=edge_all,
                scalar1=w1_edge[t],
                scalar2=b1_bf[:, t : t + 1],
                op0=MULT,
                op1=ADD,
            )

        x_codes = []
        x_scales = []
        for i in range(PIECES):
            piece_codes = const.tile([P, PIECE_PASSES * P], U32, name="x_codes%d" % i, align_bytes=64)
            piece_scales = const.tile([P, PIECE_PASSES * P], U8, name="x_scales%d" % i, align_bytes=64)
            grouped = group_piece(x_reads[i * PIECE_BANKS : (i + 1) * PIECE_BANKS])
            quantise_piece(grouped, piece_codes, piece_scales)
            x_codes.append(piece_codes)
            x_scales.append(piece_scales)
            if i == BIAS_PIECE:
                prepare_biases()
            if i >= PIECES - ORDER_LEAD:
                order_next_piece()

        pre_first = sums.tile([P, LAST, EDGES], F32)
        pre_last = sums.tile([P, 1, EDGES], F32)
        before_relu = const.tile([P, ROW_SETS, EDGES], F32)

        def add_row_sets(pre, t0, t1):
            nc.vector.tensor_tensor(out=before_relu[:, t0:t1, :], in0=pre[:], in1=added[:, t0:t1, :], op=ADD)

        def multiply_piece(n):
            t, i = w_pieces[n]
            w_codes, w_scales = quantised[n]
            for j in range(PIECE_PASSES):
                cols = slice(j * P, (j + 1) * P)
                nc.tensor.matmul_mx(
                    out=pre_last[:, 0, :] if t == LAST else pre_first[:, t, :],
                    lhsT=w_codes[:, cols].bitcast(FP8X4),
                    lhsT_scale=w_scales[:, cols],
                    rhs=x_codes[i][:, cols].bitcast(FP8X4),
                    rhs_scale=x_scales[i][:, cols],
                    start=(i == 0 and j == 0),
                    stop=(i == PIECES - 1 and j == PIECE_PASSES - 1),
                )

        quantised = []
        for r in range(rounds + MX_LAG):
            if r < rounds:
                grouped_round = []
                for n in range(r * ROUND, (r + 1) * ROUND):
                    grouped_round.append(group_piece(w_reads[n], (0,) if n == len(w_pieces) - 1 else ()))
                for n in range(r * ROUND, (r + 1) * ROUND):
                    w_codes = codes.tile([P, PIECE_PASSES * P], U32, align_bytes=64)
                    w_scales = codes.tile([P, PIECE_PASSES * P], U8, align_bytes=64)
                    calls = PIECE_BANKS if n == len(w_pieces) - 1 else 1
                    quantise_piece(grouped_round[n - r * ROUND], w_codes, w_scales, calls)
                    quantised.append((w_codes, w_scales))
                    order_next_piece()
                t, i = w_pieces[r * ROUND]
                if i + ROUND == PIECES and t < LAST:
                    prepare_added(t)
                load_next_round()
            if r >= MX_LAG:
                for n in range((r - MX_LAG) * ROUND, (r - MX_LAG + 1) * ROUND):
                    multiply_piece(n)
        prepare_added(LAST)
        add_row_sets(pre_first, 0, LAST)
        add_row_sets(pre_last, LAST, ROW_SETS)
        h_grouped = const.tile([P, EDGES, PACK], BF16, align_bytes=64)
        nc.vector.tensor_scalar_max(h_grouped[:], before_relu[:].rearrange("p t e -> p e t"), 0.0)

        scale_rows = W2_scales[0].rearrange("(q r) n -> r q n", r=4)
        for r in range(4):
            nc.sync.dma_start(out=w2_scales[r:P:32, :].bitcast(I32), in_=scale_rows[r].bitcast(I32))
        w2_codes = const.tile([P, OUT], U32, align_bytes=64)
        nc.sync.dma_start(out=w2_codes[:].bitcast(I32), in_=W2_words[0].rearrange("p n t -> p (n t)").bitcast(I32))

        h_codes = const.tile([P, EDGES], U32, align_bytes=64)
        h_scales = const.tile([P, EDGES], U8, align_bytes=64)
        nc.vector.quantize_mx(
            out=h_codes[:].bitcast(FP8X4), scales=h_scales[:], in_=h_grouped[:].rearrange("p e t -> p (e t)")
        )

        y = const.tile([P, OUT], F32)
        for start in range(0, OUT, OUT_BLOCK):
            cols = slice(start, start + OUT_BLOCK)
            product = banks.tile([P, OUT_BLOCK], F32, tag="bank")
            nc.tensor.matmul_mx(
                out=product[:],
                lhsT=h_codes[:].bitcast(FP8X4),
                lhsT_scale=h_scales[:],
                rhs=w2_codes[:, cols].bitcast(FP8X4),
                rhs_scale=w2_scales[:, cols],
                start=True,
                stop=True,
            )
            biased = results.tile([P, OUT_BLOCK], F32)
            nc.vector.tensor_tensor(out=biased[:], in0=product[:], in1=b2_all[:, cols], op=ADD)
            nc.scalar.activation(out=y[:, cols], in_=biased[:], func=TANH)
            end = start + OUT_BLOCK
            if end % STORE == 0:
                nc.sync.dma_start(out=out[:, end - STORE : end], in_=y[:, end - STORE : end])
